import numpy as np
import ml_dtypes

BF16 = ml_dtypes.bfloat16


def bf(x):
    return np.asarray(x, np.float32).astype(BF16)


def f32(x):
    return np.asarray(x, np.float32)


def f64(x):
    return np.asarray(x).astype(np.float64)


def striped(idx):
    return np.tile(idx.reshape(-1, 16).T, (8, 1))


V, D, L, T, N = 4096, 128, 2048, 3, 6144


def setup_inputs():
    sc = 1.0 / np.sqrt(D)
    return {
        "table": bf(np.random.standard_normal((D, V))),
        "wc": bf(sc * np.random.standard_normal((D, D))),
        "bc": f32(0.1 * np.random.standard_normal((D, 1))),
        "wq": bf(sc * np.random.standard_normal((D, D))),
        "wk": bf(sc * np.random.standard_normal((D, D))),
        "wv": bf(sc * np.random.standard_normal((D, D))),
        "wo": bf(sc * np.random.standard_normal((D, D))),
        "mask": f32(np.maximum(np.random.random((L, L)) < 0.5, np.eye(L))),
        "offs": striped(np.random.permutation(np.tile(np.arange(V), 2))[:N]),
    }


def reference(table, wc, bc, wq, wk, wv, wo, mask, offs):
    idx = offs[:16].T.reshape(-1)
    e = f64(wc).T @ f64(table)[:, idx] + f64(bc)
    e3 = e.reshape(D, T, L)
    root = e3.sum(axis=1)
    enc = np.maximum(np.maximum(root, e3[:, 1:].max(axis=1)), 0.0)
    q = f64(wq).T @ enc
    k = f64(wk).T @ enc
    v = f64(wv).T @ enc
    s = (k.T @ q) / np.sqrt(D)
    p = f64(mask) * np.exp(s)
    ctx = (v @ p) / p.sum(axis=0, keepdims=True)
    return f64(wo).T @ ctx

@@ -1,0 +1,195 @@
+import math
+
+import concourse.mybir as mybir
+from concourse.masks import make_identity
+
+BF16 = mybir.dt.bfloat16
+F32 = mybir.dt.float32
+U16 = mybir.dt.uint16
+ADD = mybir.AluOpType.add
+MAX = mybir.AluOpType.max
+MULT = mybir.AluOpType.mult
+IDENTITY = mybir.ActivationFunctionType.Identity
+EXP = mybir.ActivationFunctionType.Exp
+
+P = 128
+V = 4096
+L = 2048
+NODES = 3
+CHUNK = 512
+N_CHUNKS = L // CHUNK
+BLOCKS = CHUNK // P
+N_BLOCKS = L // P
+OFFS_COLS = CHUNK // 16
+V_ONE = P + 1
+N_TILES = N_CHUNKS * N_BLOCKS
+V_PITCH = 144
+
+AHEAD = 3
+FLIP_AFTER = 2
+OUT_AFTER = 4
+
+FLOPS = 2 * P * P * NODES * L + 3 * 2 * P * P * L + 2 * 2 * P * L * L + 2 * P * P * L
+
+
+def tile_batchprogramclassifier_b_kernel(tc, table, wc, bc, wq, wk, wv, wo, mask, offs, out):
+    nc = tc.nc
+    with (
+        tc.tile_pool(name="held", bufs=1) as held,
+        tc.tile_pool(name="work", bufs=2) as work,
+        tc.tile_pool(name="probs", bufs=AHEAD + 2) as probs,
+        tc.psum_pool(name="banks", bufs=8) as banks,
+    ):
+        offsets = held.tile([P, NODES * L // 16], U16, name="offsets")
+        nc.sync.dma_start(offsets[:], offs)
+        table_sb = held.tile([P, V], BF16, name="table_sb")
+        nc.sync.dma_start(table_sb[:], table)
+
+        weights = {}
+        for name, w in (("wc", wc), ("wq", wq), ("wk", wk), ("wv", wv), ("wo", wo)):
+            weights[name] = held.tile([P, P], BF16, name=name + "_sb")
+            nc.scalar.dma_start(weights[name][:], w)
+        bc_sb = held.tile([P, 1], F32, name="bc_sb")
+        nc.scalar.dma_start(bc_sb[:], bc)
+
+        mask_view = mask.rearrange("(g j p) l -> g p j l", j=BLOCKS, p=P)
+        mask_sb = []
+        for c in range(N_CHUNKS):
+            mask_sb.append([])
+            for g in range(N_BLOCKS // BLOCKS):
+                m_tile = held.tile([P, BLOCKS, CHUNK], F32, name=f"mask_{c}_{g}")
+                nc.sync.dma_start(m_tile[:], mask_view[g, :, :, c * CHUNK : (c + 1) * CHUNK])
+                mask_sb[c].append(m_tile)
+
+        identity = held.tile([P, P], BF16, name="identity")
+        make_identity(nc, identity[:])
+
+        enc = held.tile([P, L], BF16, name="enc")
+        q = held.tile([P, L], BF16, name="q")
+        k = held.tile([P, L], BF16, name="k")
+        v_one = held.tile([P, N_BLOCKS, V_PITCH], BF16, name="v_one")
+        nc.vector.memset(v_one[:, :, P:V_ONE], 1.0)
+
+        def chunk_cols(c):
+            return slice(c * CHUNK, (c + 1) * CHUNK)
+
+        def bank(shape, dtype, name):
+            return banks.tile(shape, dtype, name=name, tag="bank")
+
+        def embed(c):
+            raw = {}
+            for node in (1, 2, 0):
+                piece = node * N_CHUNKS + c
+                raw[node] = bank([P, CHUNK], F32, f"raw{node}")
+                nc.tensor.matmul(
+                    raw[node][:],
+                    weights["wc"][:],
+                    table_sb[:].indirect(offsets[:, piece * OFFS_COLS : (piece + 1) * OFFS_COLS]),
+                    start=True,
+                    stop=True,
+                )
+            return raw
+
+        def pool_trees(c, raw):
+            left = work.tile([P, CHUNK], F32, name="left")
+            nc.scalar.activation(left[:], raw[1][:], IDENTITY, bias=bc_sb[:, 0:1])
+            children = work.tile([P, CHUNK], F32, name="children")
+            nc.vector.scalar_tensor_tensor(children[:], raw[2][:], bc_sb[:, 0:1], left[:], ADD, ADD)
+            biggest = work.tile([P, CHUNK], F32, name="biggest")
+            nc.vector.scalar_tensor_tensor(biggest[:], raw[2][:], bc_sb[:, 0:1], left[:], ADD, MAX)
+            subtree = work.tile([P, CHUNK], F32, name="subtree")
+            nc.vector.scalar_tensor_tensor(subtree[:], raw[0][:], bc_sb[:, 0:1], children[:], ADD, ADD)
+            nc.vector.scalar_tensor_tensor(enc[:, chunk_cols(c)], subtree[:], 0.0, biggest[:], MAX, MAX)
+
+        def project(w_name, dest, c):
+            proj = bank([P, CHUNK], F32, "proj")
+            nc.tensor.matmul(proj[:], weights[w_name][:], enc[:, chunk_cols(c)], start=True, stop=True)
+            nc.scalar.copy(dest[:, chunk_cols(c)], proj[:])
+
+        def project_v(c):
+            v_t = bank([P, BLOCKS, P], F32, "v_t")
+            for j in range(BLOCKS):
+                block = c * BLOCKS + j
+                nc.tensor.matmul(
+                    v_t[:, j, :], enc[:, block * P : (block + 1) * P], weights["wv"][:], start=True, stop=True
+                )
+            nc.scalar.copy(v_one[:, c * BLOCKS : (c + 1) * BLOCKS, 0:P], v_t[:])
+
+        def exp_scores(c, t):
+            scores = bank([P, CHUNK], F32, "scores")
+            nc.tensor.matmul(scores[:], k[:, t * P : (t + 1) * P], q[:, chunk_cols(c)], start=True, stop=True)
+            e = probs.tile([P, CHUNK], BF16, name="e")
+            nc.scalar.activation(e[:], scores[:], EXP, scale=1.0 / math.sqrt(P))
+            return e
+
+        def attend(c, t, e, ctx_den):
+            p = probs.tile([P, CHUNK], BF16, name="p")
+            nc.vector.tensor_tensor(p[:], e[:], mask_sb[c][t // BLOCKS][:, t % BLOCKS, :], MULT)
+            for b in range(BLOCKS):
+                nc.tensor.matmul(
+                    ctx_den[b][:],
+                    p[:, b * P : (b + 1) * P],
+                    v_one[:, t, 0:V_ONE],
+                    start=(t == 0),
+                    stop=(t == N_BLOCKS - 1),
+                )
+
+        def normalise(ctx_den):
+            ctx_t = work.tile([P, BLOCKS, P], BF16, name="ctx_t")
+            for b in range(BLOCKS):
+                inv_den = work.tile([P, 1], F32, name="inv_den")
+                nc.vector.reciprocal(inv_den[:], ctx_den[b][:, P:V_ONE])
+                nc.vector.tensor_scalar_mul(ctx_t[:, b, :], ctx_den[b][:, 0:P], inv_den[:, 0:1])
+            return ctx_t
+
+        def flip(ctx_t):
+            flipped = bank([P, CHUNK], BF16, "flipped")
+            for b in range(BLOCKS):
+                nc.tensor.transpose(flipped[:, b * P : (b + 1) * P], ctx_t[:, b, :], identity[:])
+            ctx = work.tile([P, CHUNK], BF16, name="ctx")
+            nc.vector.tensor_copy(ctx[:], flipped[:])
+            return ctx
+
+        def project_out(c, ctx):
+            result = bank([P, CHUNK], F32, "result")
+            nc.tensor.matmul(result[:], weights["wo"][:], ctx[:], start=True, stop=True)
+            out_sb = work.tile([P, CHUNK], F32, name="out_sb")
+            nc.scalar.copy(out_sb[:], result[:])
+            nc.sync.dma_start(out[:, chunk_cols(c)], out_sb[:])
+
+        raw = {}
+        for c in range(N_CHUNKS + 1):
+            if c < N_CHUNKS:
+                raw[c] = embed(c)
+            if c >= 1:
+                pool_trees(c - 1, raw[c - 1])
+
+        project("wq", q, 0)
+        project("wk", k, 0)
+        project_v(0)
+        e_tiles, ctx_den, ctx_t, ctx = {}, {}, {}, {}
+        for step in range(N_TILES + AHEAD + OUT_AFTER):
+            if step < N_TILES:
+                c, t = divmod(step, N_BLOCKS)
+                if c == 0 and t % BLOCKS == 0 and t // BLOCKS + 1 < N_CHUNKS:
+                    project("wk", k, t // BLOCKS + 1)
+                    project_v(t // BLOCKS + 1)
+                if t == N_BLOCKS // 2 and c + 1 < N_CHUNKS:
+                    project("wq", q, c + 1)
+                e_tiles[step] = exp_scores(c, t)
+
+            c, t = divmod(step - AHEAD, N_BLOCKS)
+            if 0 <= c < N_CHUNKS:
+                if t == 0:
+                    ctx_den[c] = [bank([P, V_ONE], F32, f"ctx_den{b}") for b in range(BLOCKS)]
+                attend(c, t, e_tiles[step - AHEAD], ctx_den[c])
+                if t == N_BLOCKS - 1:
+                    ctx_t[c] = normalise(ctx_den[c])
+
+            c, t = divmod(step - AHEAD - FLIP_AFTER, N_BLOCKS)
+            if 0 <= c < N_CHUNKS and t == N_BLOCKS - 1:
+                ctx[c] = flip(ctx_t[c])
+
+            c, t = divmod(step - AHEAD - OUT_AFTER, N_BLOCKS)
+            if 0 <= c < N_CHUNKS and t == N_BLOCKS - 1:
+                project_out(c, ctx[c])

@@ -24,10 +24,14 @@ OFFS_COLS = CHUNK // 16
 V_ONE = P + 1
 N_TILES = N_CHUNKS * N_BLOCKS
 V_PITCH = 144
+PER_BANK = 2
 
 AHEAD = 3
-FLIP_AFTER = 2
-OUT_AFTER = 4
+NORMALISE_AFTER = 2
+FLIP_AFTER = 3
+UNLOAD_AFTER = 5
+PROJECT_AFTER = 6
+STORE_AFTER = 7
 
 FLOPS = 2 * P * P * NODES * L + 3 * 2 * P * P * L + 2 * 2 * P * L * L + 2 * P * P * L
 
@@ -122,40 +126,52 @@ def tile_batchprogramclassifier_b_kernel(tc, table, wc, bc, wq, wk, wv, wo, mask
             nc.scalar.activation(e[:], scores[:], EXP, scale=1.0 / math.sqrt(P))
             return e
 
-        def attend(c, t, e, ctx_den):
+        def attend(c, t, e, sums):
             p = probs.tile([P, CHUNK], BF16, name="p")
             nc.vector.tensor_tensor(p[:], e[:], mask_sb[c][t // BLOCKS][:, t % BLOCKS, :], MULT)
             for b in range(BLOCKS):
+                half, place = divmod(b, PER_BANK)
                 nc.tensor.matmul(
-                    ctx_den[b][:],
+                    sums[half][:, place, :],
                     p[:, b * P : (b + 1) * P],
                     v_one[:, t, 0:V_ONE],
-                    start=(t == 0),
-                    stop=(t == N_BLOCKS - 1),
+                    start=(t == 0 and place == 0),
+                    stop=(t == N_BLOCKS - 1 and place == PER_BANK - 1),
                 )
 
-        def normalise(ctx_den):
+        def normalise(sums):
             ctx_t = work.tile([P, BLOCKS, P], BF16, name="ctx_t")
+            inv_den = work.tile([P, BLOCKS, 1], F32, name="inv_den")
             for b in range(BLOCKS):
-                inv_den = work.tile([P, 1], F32, name="inv_den")
-                nc.vector.reciprocal(inv_den[:], ctx_den[b][:, P:V_ONE])
-                nc.vector.tensor_scalar_mul(ctx_t[:, b, :], ctx_den[b][:, 0:P], inv_den[:, 0:1])
+                half, place = divmod(b, PER_BANK)
+                nc.vector.reciprocal(inv_den[:, b, :], sums[half][:, place, P:V_ONE])
+                nc.vector.tensor_scalar_mul(ctx_t[:, b, :], sums[half][:, place, 0:P], inv_den[:, b, :])
             return ctx_t
 
         def flip(ctx_t):
             flipped = bank([P, CHUNK], BF16, "flipped")
             for b in range(BLOCKS):
                 nc.tensor.transpose(flipped[:, b * P : (b + 1) * P], ctx_t[:, b, :], identity[:])
+            return flipped
+
+        def unload(flipped):
             ctx = work.tile([P, CHUNK], BF16, name="ctx")
             nc.vector.tensor_copy(ctx[:], flipped[:])
             return ctx
 
-        def project_out(c, ctx):
+        def project_out(ctx):
             result = bank([P, CHUNK], F32, "result")
             nc.tensor.matmul(result[:], weights["wo"][:], ctx[:], start=True, stop=True)
+            return result
+
+        def store(c, result):
             out_sb = work.tile([P, CHUNK], F32, name="out_sb")
             nc.scalar.copy(out_sb[:], result[:])
             nc.sync.dma_start(out[:, chunk_cols(c)], out_sb[:])
+
+        def chunk_done(step, after):
+            c, t = divmod(step - AHEAD - after, N_BLOCKS)
+            return c if t == N_BLOCKS - 1 and 0 <= c < N_CHUNKS else None
 
         raw = {}
         for c in range(N_CHUNKS + 1):
@@ -167,8 +183,8 @@ def tile_batchprogramclassifier_b_kernel(tc, table, wc, bc, wq, wk, wv, wo, mask
         project("wq", q, 0)
         project("wk", k, 0)
         project_v(0)
-        e_tiles, ctx_den, ctx_t, ctx = {}, {}, {}, {}
-        for step in range(N_TILES + AHEAD + OUT_AFTER):
+        e_tiles, sums, ctx_t, flipped, ctx, result = {}, {}, {}, {}, {}, {}
+        for step in range(N_TILES + AHEAD + STORE_AFTER):
             if step < N_TILES:
                 c, t = divmod(step, N_BLOCKS)
                 if c == 0 and t % BLOCKS == 0 and t // BLOCKS + 1 < N_CHUNKS:
@@ -181,15 +197,21 @@ def tile_batchprogramclassifier_b_kernel(tc, table, wc, bc, wq, wk, wv, wo, mask
             c, t = divmod(step - AHEAD, N_BLOCKS)
             if 0 <= c < N_CHUNKS:
                 if t == 0:
-                    ctx_den[c] = [bank([P, V_ONE], F32, f"ctx_den{b}") for b in range(BLOCKS)]
-                attend(c, t, e_tiles[step - AHEAD], ctx_den[c])
-                if t == N_BLOCKS - 1:
-                    ctx_t[c] = normalise(ctx_den[c])
+                    sums[c] = [bank([P, PER_BANK, V_ONE], F32, f"sums{h}") for h in range(BLOCKS // PER_BANK)]
+                attend(c, t, e_tiles[step - AHEAD], sums[c])
 
-            c, t = divmod(step - AHEAD - FLIP_AFTER, N_BLOCKS)
-            if 0 <= c < N_CHUNKS and t == N_BLOCKS - 1:
-                ctx[c] = flip(ctx_t[c])
-
-            c, t = divmod(step - AHEAD - OUT_AFTER, N_BLOCKS)
-            if 0 <= c < N_CHUNKS and t == N_BLOCKS - 1:
-                project_out(c, ctx[c])
+            c = chunk_done(step, NORMALISE_AFTER)
+            if c is not None:
+                ctx_t[c] = normalise(sums[c])
+            c = chunk_done(step, FLIP_AFTER)
+            if c is not None:
+                flipped[c] = flip(ctx_t[c])
+            c = chunk_done(step, UNLOAD_AFTER)
+            if c is not None:
+                ctx[c] = unload(flipped[c])
+            c = chunk_done(step, PROJECT_AFTER)
+            if c is not None:
+                result[c] = project_out(ctx[c])
+            c = chunk_done(step, STORE_AFTER)
+            if c is not None:
+                store(c, result[c])

@@ -26,7 +26,7 @@ N_TILES = N_CHUNKS * N_BLOCKS
 V_PITCH = 144
 PER_BANK = 2
 
-AHEAD = 3
+AHEAD = 5
 NORMALISE_AFTER = 2
 FLIP_AFTER = 3
 UNLOAD_AFTER = 5
@@ -55,6 +55,10 @@ def tile_batchprogramclassifier_b_kernel(tc, table, wc, bc, wq, wk, wv, wo, mask
             nc.scalar.dma_start(weights[name][:], w)
         bc_sb = held.tile([P, 1], F32, name="bc_sb")
         nc.scalar.dma_start(bc_sb[:], bc)
+
+        warm = held.tile([P, 1], F32, name="warm")
+        nc.vector.memset(warm[:], 0.0)
+        nc.scalar.activation(warm[:], warm[:], EXP)
 
         mask_view = mask.rearrange("(g j p) l -> g p j l", j=BLOCKS, p=P)
         mask_sb = []

@@ -110,12 +110,12 @@ def tile_batchprogramclassifier_b_kernel(tc, table, wc, bc, wq, wk, wv, wo, mask
             nc.vector.scalar_tensor_tensor(enc[:, chunk_cols(c)], subtree[:], 0.0, biggest[:], MAX, MAX)
 
         def project(w_name, dest, c):
-            proj = bank([P, CHUNK], F32, "proj")
+            proj = bank([P, CHUNK], BF16, "proj")
             nc.tensor.matmul(proj[:], weights[w_name][:], enc[:, chunk_cols(c)], start=True, stop=True)
             nc.scalar.copy(dest[:, chunk_cols(c)], proj[:])
 
         def project_v(c):
-            v_t = bank([P, BLOCKS, P], F32, "v_t")
+            v_t = bank([P, BLOCKS, P], BF16, "v_t")
             for j in range(BLOCKS):
                 block = c * BLOCKS + j
                 nc.tensor.matmul(

@@ -27,6 +27,7 @@ V_PITCH = 144
 PER_BANK = 2
 
 AHEAD = 5
+WARM_UP = 24
 NORMALISE_AFTER = 2
 FLIP_AFTER = 3
 UNLOAD_AFTER = 5
@@ -176,6 +177,10 @@ def tile_batchprogramclassifier_b_kernel(tc, table, wc, bc, wq, wk, wv, wo, mask
         def chunk_done(step, after):
             c, t = divmod(step - AHEAD - after, N_BLOCKS)
             return c if t == N_BLOCKS - 1 and 0 <= c < N_CHUNKS else None
+
+        spin = bank([P, P], F32, "spin")
+        for turn in range(WARM_UP):
+            nc.tensor.matmul(spin[:], identity[:], identity[:], start=True, stop=True)
 
         raw = {}
         for c in range(N_CHUNKS + 1):

@@ -27,7 +27,7 @@ V_PITCH = 144
 PER_BANK = 2
 
 AHEAD = 5
-WARM_UP = 24
+V_UNLOAD_AFTER = 2
 NORMALISE_AFTER = 2
 FLIP_AFTER = 3
 UNLOAD_AFTER = 5
@@ -102,8 +102,10 @@ def tile_batchprogramclassifier_b_kernel(tc, table, wc, bc, wq, wk, wv, wo, mask
         def pool_trees(c, raw):
             left = work.tile([P, CHUNK], F32, name="left")
             nc.scalar.activation(left[:], raw[1][:], IDENTITY, bias=bc_sb[:, 0:1])
+            right = work.tile([P, CHUNK], F32, name="right")
+            nc.scalar.activation(right[:], raw[2][:], IDENTITY, bias=bc_sb[:, 0:1])
             children = work.tile([P, CHUNK], F32, name="children")
-            nc.vector.scalar_tensor_tensor(children[:], raw[2][:], bc_sb[:, 0:1], left[:], ADD, ADD)
+            nc.gpsimd.tensor_tensor(children[:], left[:], right[:], ADD)
             biggest = work.tile([P, CHUNK], F32, name="biggest")
             nc.vector.scalar_tensor_tensor(biggest[:], raw[2][:], bc_sb[:, 0:1], left[:], ADD, MAX)
             subtree = work.tile([P, CHUNK], F32, name="subtree")
@@ -122,7 +124,10 @@ def tile_batchprogramclassifier_b_kernel(tc, table, wc, bc, wq, wk, wv, wo, mask
                 nc.tensor.matmul(
                     v_t[:, j, :], enc[:, block * P : (block + 1) * P], weights["wv"][:], start=True, stop=True
                 )
-            nc.scalar.copy(v_one[:, c * BLOCKS : (c + 1) * BLOCKS, 0:P], v_t[:])
+            return v_t
+
+        def unload_v(c, v_t):
+            nc.vector.tensor_copy(v_one[:, c * BLOCKS : (c + 1) * BLOCKS, 0:P], v_t[:])
 
         def exp_scores(c, t):
             scores = bank([P, CHUNK], F32, "scores")
@@ -178,10 +183,6 @@ def tile_batchprogramclassifier_b_kernel(tc, table, wc, bc, wq, wk, wv, wo, mask
             c, t = divmod(step - AHEAD - after, N_BLOCKS)
             return c if t == N_BLOCKS - 1 and 0 <= c < N_CHUNKS else None
 
-        spin = bank([P, P], F32, "spin")
-        for turn in range(WARM_UP):
-            nc.tensor.matmul(spin[:], identity[:], identity[:], start=True, stop=True)
-
         raw = {}
         for c in range(N_CHUNKS + 1):
             if c < N_CHUNKS:
@@ -191,14 +192,15 @@ def tile_batchprogramclassifier_b_kernel(tc, table, wc, bc, wq, wk, wv, wo, mask
 
         project("wq", q, 0)
         project("wk", k, 0)
-        project_v(0)
+        unload_v(0, project_v(0))
+        v_tiles = {}
         e_tiles, sums, ctx_t, flipped, ctx, result = {}, {}, {}, {}, {}, {}
         for step in range(N_TILES + AHEAD + STORE_AFTER):
             if step < N_TILES:
                 c, t = divmod(step, N_BLOCKS)
                 if c == 0 and t % BLOCKS == 0 and t // BLOCKS + 1 < N_CHUNKS:
                     project("wk", k, t // BLOCKS + 1)
-                    project_v(t // BLOCKS + 1)
+                    v_tiles[t // BLOCKS + 1] = project_v(t // BLOCKS + 1)
                 if t == N_BLOCKS // 2 and c + 1 < N_CHUNKS:
                     project("wq", q, c + 1)
                 e_tiles[step] = exp_scores(c, t)
@@ -208,6 +210,10 @@ def tile_batchprogramclassifier_b_kernel(tc, table, wc, bc, wq, wk, wv, wo, mask
                 if t == 0:
                     sums[c] = [bank([P, PER_BANK, V_ONE], F32, f"sums{h}") for h in range(BLOCKS // PER_BANK)]
                 attend(c, t, e_tiles[step - AHEAD], sums[c])
+
+            g, t = divmod(step - V_UNLOAD_AFTER, BLOCKS)
+            if t == 0 and 0 <= g < N_CHUNKS - 1:
+                unload_v(g + 1, v_tiles[g + 1])
 
             c = chunk_done(step, NORMALISE_AFTER)
             if c is not None:

@@ -27,7 +27,6 @@ V_PITCH = 144
 PER_BANK = 2
 
 AHEAD = 5
-V_UNLOAD_AFTER = 2
 NORMALISE_AFTER = 2
 FLIP_AFTER = 3
 UNLOAD_AFTER = 5
@@ -102,10 +101,8 @@ def tile_batchprogramclassifier_b_kernel(tc, table, wc, bc, wq, wk, wv, wo, mask
         def pool_trees(c, raw):
             left = work.tile([P, CHUNK], F32, name="left")
             nc.scalar.activation(left[:], raw[1][:], IDENTITY, bias=bc_sb[:, 0:1])
-            right = work.tile([P, CHUNK], F32, name="right")
-            nc.scalar.activation(right[:], raw[2][:], IDENTITY, bias=bc_sb[:, 0:1])
             children = work.tile([P, CHUNK], F32, name="children")
-            nc.gpsimd.tensor_tensor(children[:], left[:], right[:], ADD)
+            nc.vector.scalar_tensor_tensor(children[:], raw[2][:], bc_sb[:, 0:1], left[:], ADD, ADD)
             biggest = work.tile([P, CHUNK], F32, name="biggest")
             nc.vector.scalar_tensor_tensor(biggest[:], raw[2][:], bc_sb[:, 0:1], left[:], ADD, MAX)
             subtree = work.tile([P, CHUNK], F32, name="subtree")
@@ -124,10 +121,7 @@ def tile_batchprogramclassifier_b_kernel(tc, table, wc, bc, wq, wk, wv, wo, mask
                 nc.tensor.matmul(
                     v_t[:, j, :], enc[:, block * P : (block + 1) * P], weights["wv"][:], start=True, stop=True
                 )
-            return v_t
-
-        def unload_v(c, v_t):
-            nc.vector.tensor_copy(v_one[:, c * BLOCKS : (c + 1) * BLOCKS, 0:P], v_t[:])
+            nc.scalar.copy(v_one[:, c * BLOCKS : (c + 1) * BLOCKS, 0:P], v_t[:])
 
         def exp_scores(c, t):
             scores = bank([P, CHUNK], F32, "scores")
@@ -152,10 +146,12 @@ def tile_batchprogramclassifier_b_kernel(tc, table, wc, bc, wq, wk, wv, wo, mask
         def normalise(sums):
             ctx_t = work.tile([P, BLOCKS, P], BF16, name="ctx_t")
             inv_den = work.tile([P, BLOCKS, 1], F32, name="inv_den")
-            for b in range(BLOCKS):
-                half, place = divmod(b, PER_BANK)
-                nc.vector.reciprocal(inv_den[:, b, :], sums[half][:, place, P:V_ONE])
-                nc.vector.tensor_scalar_mul(ctx_t[:, b, :], sums[half][:, place, 0:P], inv_den[:, b, :])
+            for half in range(BLOCKS // PER_BANK):
+                both = slice(half * PER_BANK, (half + 1) * PER_BANK)
+                nc.vector.reciprocal(inv_den[:, both, :], sums[half][:, :, P:V_ONE])
+                nc.vector.tensor_tensor(
+                    ctx_t[:, both, :], sums[half][:, :, 0:P], inv_den[:, both, :].to_broadcast([P, PER_BANK, P]), MULT
+                )
             return ctx_t
 
         def flip(ctx_t):
@@ -192,15 +188,14 @@ def tile_batchprogramclassifier_b_kernel(tc, table, wc, bc, wq, wk, wv, wo, mask
 
         project("wq", q, 0)
         project("wk", k, 0)
-        unload_v(0, project_v(0))
-        v_tiles = {}
+        project_v(0)
         e_tiles, sums, ctx_t, flipped, ctx, result = {}, {}, {}, {}, {}, {}
         for step in range(N_TILES + AHEAD + STORE_AFTER):
             if step < N_TILES:
                 c, t = divmod(step, N_BLOCKS)
                 if c == 0 and t % BLOCKS == 0 and t // BLOCKS + 1 < N_CHUNKS:
                     project("wk", k, t // BLOCKS + 1)
-                    v_tiles[t // BLOCKS + 1] = project_v(t // BLOCKS + 1)
+                    project_v(t // BLOCKS + 1)
                 if t == N_BLOCKS // 2 and c + 1 < N_CHUNKS:
                     project("wq", q, c + 1)
                 e_tiles[step] = exp_scores(c, t)
@@ -210,10 +205,6 @@ def tile_batchprogramclassifier_b_kernel(tc, table, wc, bc, wq, wk, wv, wo, mask
                 if t == 0:
                     sums[c] = [bank([P, PER_BANK, V_ONE], F32, f"sums{h}") for h in range(BLOCKS // PER_BANK)]
                 attend(c, t, e_tiles[step - AHEAD], sums[c])
-
-            g, t = divmod(step - V_UNLOAD_AFTER, BLOCKS)
-            if t == 0 and 0 <= g < N_CHUNKS - 1:
-                unload_v(g + 1, v_tiles[g + 1])
 
             c = chunk_done(step, NORMALISE_AFTER)
             if c is not None:

@@ -11,6 +11,7 @@ MAX = mybir.AluOpType.max
 MULT = mybir.AluOpType.mult
 IDENTITY = mybir.ActivationFunctionType.Identity
 EXP = mybir.ActivationFunctionType.Exp
+RELU = mybir.ActivationFunctionType.Relu
 
 P = 128
 V = 4096
@@ -101,13 +102,15 @@ def tile_batchprogramclassifier_b_kernel(tc, table, wc, bc, wq, wk, wv, wo, mask
         def pool_trees(c, raw):
             left = work.tile([P, CHUNK], F32, name="left")
             nc.scalar.activation(left[:], raw[1][:], IDENTITY, bias=bc_sb[:, 0:1])
+            left_or_zero = work.tile([P, CHUNK], BF16, name="left_or_zero")
+            nc.scalar.activation(left_or_zero[:], raw[1][:], RELU, bias=bc_sb[:, 0:1])
             children = work.tile([P, CHUNK], F32, name="children")
             nc.vector.scalar_tensor_tensor(children[:], raw[2][:], bc_sb[:, 0:1], left[:], ADD, ADD)
-            biggest = work.tile([P, CHUNK], F32, name="biggest")
-            nc.vector.scalar_tensor_tensor(biggest[:], raw[2][:], bc_sb[:, 0:1], left[:], ADD, MAX)
-            subtree = work.tile([P, CHUNK], F32, name="subtree")
+            biggest = work.tile([P, CHUNK], BF16, name="biggest")
+            nc.vector.scalar_tensor_tensor(biggest[:], raw[2][:], bc_sb[:, 0:1], left_or_zero[:], ADD, MAX)
+            subtree = work.tile([P, CHUNK], BF16, name="subtree")
             nc.vector.scalar_tensor_tensor(subtree[:], raw[0][:], bc_sb[:, 0:1], children[:], ADD, ADD)
-            nc.vector.scalar_tensor_tensor(enc[:, chunk_cols(c)], subtree[:], 0.0, biggest[:], MAX, MAX)
+            nc.vector.tensor_tensor(enc[:, chunk_cols(c)], subtree[:], biggest[:], MAX)
 
         def project(w_name, dest, c):
             proj = bank([P, CHUNK], BF16, "proj")

@@ -33,6 +33,7 @@ FLIP_AFTER = 3
 UNLOAD_AFTER = 5
 PROJECT_AFTER = 6
 STORE_AFTER = 7
+COPY_AFTER = 2
 
 FLOPS = 2 * P * P * NODES * L + 3 * 2 * P * P * L + 2 * 2 * P * L * L + 2 * P * P * L
 
@@ -112,10 +113,10 @@ def tile_batchprogramclassifier_b_kernel(tc, table, wc, bc, wq, wk, wv, wo, mask
             nc.vector.scalar_tensor_tensor(subtree[:], raw[0][:], bc_sb[:, 0:1], children[:], ADD, ADD)
             nc.vector.tensor_tensor(enc[:, chunk_cols(c)], subtree[:], biggest[:], MAX)
 
-        def project(w_name, dest, c):
+        def project(w_name, c):
             proj = bank([P, CHUNK], BF16, "proj")
             nc.tensor.matmul(proj[:], weights[w_name][:], enc[:, chunk_cols(c)], start=True, stop=True)
-            nc.scalar.copy(dest[:, chunk_cols(c)], proj[:])
+            return proj
 
         def project_v(c):
             v_t = bank([P, BLOCKS, P], BF16, "v_t")
@@ -124,7 +125,10 @@ def tile_batchprogramclassifier_b_kernel(tc, table, wc, bc, wq, wk, wv, wo, mask
                 nc.tensor.matmul(
                     v_t[:, j, :], enc[:, block * P : (block + 1) * P], weights["wv"][:], start=True, stop=True
                 )
-            nc.scalar.copy(v_one[:, c * BLOCKS : (c + 1) * BLOCKS, 0:P], v_t[:])
+            return v_t
+
+        def keep_v(c, v_t):
+            nc.vector.tensor_copy(v_one[:, c * BLOCKS : (c + 1) * BLOCKS, 0:P], v_t[:])
 
         def exp_scores(c, t):
             scores = bank([P, CHUNK], F32, "scores")
@@ -189,18 +193,25 @@ def tile_batchprogramclassifier_b_kernel(tc, table, wc, bc, wq, wk, wv, wo, mask
             if c >= 1:
                 pool_trees(c - 1, raw[c - 1])
 
-        project("wq", q, 0)
-        project("wk", k, 0)
-        project_v(0)
-        e_tiles, sums, ctx_t, flipped, ctx, result = {}, {}, {}, {}, {}, {}
+        nc.scalar.copy(q[:, chunk_cols(0)], project("wq", 0)[:])
+        nc.scalar.copy(k[:, chunk_cols(0)], project("wk", 0)[:])
+        keep_v(0, project_v(0))
+        e_tiles, sums, ctx_t, flipped, ctx, result, v_ps, q_ps = {}, {}, {}, {}, {}, {}, {}, {}
         for step in range(N_TILES + AHEAD + STORE_AFTER):
             if step < N_TILES:
                 c, t = divmod(step, N_BLOCKS)
-                if c == 0 and t % BLOCKS == 0 and t // BLOCKS + 1 < N_CHUNKS:
-                    project("wk", k, t // BLOCKS + 1)
-                    project_v(t // BLOCKS + 1)
-                if t == N_BLOCKS // 2 and c + 1 < N_CHUNKS:
-                    project("wq", q, c + 1)
+                coming = t // BLOCKS + 1
+                if c == 0 and coming < N_CHUNKS:
+                    if t % BLOCKS == 0:
+                        nc.scalar.copy(k[:, chunk_cols(coming)], project("wk", coming)[:])
+                        v_ps[coming] = project_v(coming)
+                    if t % BLOCKS == COPY_AFTER:
+                        keep_v(coming, v_ps[coming])
+                if c + 1 < N_CHUNKS:
+                    if t == N_BLOCKS // 2:
+                        q_ps[c + 1] = project("wq", c + 1)
+                    if t == N_BLOCKS // 2 + COPY_AFTER:
+                        nc.vector.tensor_copy(q[:, chunk_cols(c + 1)], q_ps[c + 1][:])
                 e_tiles[step] = exp_scores(c, t)
 
             c, t = divmod(step - AHEAD, N_BLOCKS)

@@ -12,6 +12,7 @@ MULT = mybir.AluOpType.mult
 IDENTITY = mybir.ActivationFunctionType.Identity
 EXP = mybir.ActivationFunctionType.Exp
 RELU = mybir.ActivationFunctionType.Relu
+COPY = mybir.ActivationFunctionType.Copy
 
 P = 128
 V = 4096
@@ -25,9 +26,10 @@ OFFS_COLS = CHUNK // 16
 V_ONE = P + 1
 N_TILES = N_CHUNKS * N_BLOCKS
 V_PITCH = 144
+HALF = 2 * P
 PER_BANK = 2
 
-AHEAD = 5
+AHEAD = 7
 NORMALISE_AFTER = 2
 FLIP_AFTER = 3
 UNLOAD_AFTER = 5
@@ -150,37 +152,46 @@ def tile_batchprogramclassifier_b_kernel(tc, table, wc, bc, wq, wk, wv, wo, mask
                     stop=(t == N_BLOCKS - 1 and place == PER_BANK - 1),
                 )
 
-        def normalise(sums):
-            ctx_t = work.tile([P, BLOCKS, P], BF16, name="ctx_t")
-            inv_den = work.tile([P, BLOCKS, 1], F32, name="inv_den")
-            for half in range(BLOCKS // PER_BANK):
-                both = slice(half * PER_BANK, (half + 1) * PER_BANK)
-                nc.vector.reciprocal(inv_den[:, both, :], sums[half][:, :, P:V_ONE])
+        def normalise(half, bank_sums):
+            ctx_t = work.tile([P, PER_BANK, P], BF16, name=f"ctx_t{half}")
+            inv_den = work.tile([P, PER_BANK, 1], F32, name=f"inv_den{half}")
+            nc.vector.reciprocal(inv_den[:], bank_sums[:, :, P:V_ONE])
+            if half == 0:
                 nc.vector.tensor_tensor(
-                    ctx_t[:, both, :], sums[half][:, :, 0:P], inv_den[:, both, :].to_broadcast([P, PER_BANK, P]), MULT
+                    ctx_t[:], bank_sums[:, :, 0:P], inv_den[:].to_broadcast([P, PER_BANK, P]), MULT
                 )
+            else:
+                for place in range(PER_BANK):
+                    nc.scalar.activation(ctx_t[:, place, :], bank_sums[:, place, 0:P], COPY, scale=inv_den[:, place, :])
             return ctx_t
 
         def flip(ctx_t):
-            flipped = bank([P, CHUNK], BF16, "flipped")
-            for b in range(BLOCKS):
-                nc.tensor.transpose(flipped[:, b * P : (b + 1) * P], ctx_t[:, b, :], identity[:])
+            flipped = bank([P, HALF], BF16, "flipped")
+            for place in range(PER_BANK):
+                nc.tensor.transpose(flipped[:, place * P : (place + 1) * P], ctx_t[:, place, :], identity[:])
             return flipped
 
-        def unload(flipped):
-            ctx = work.tile([P, CHUNK], BF16, name="ctx")
-            nc.vector.tensor_copy(ctx[:], flipped[:])
+        def unload(half, flipped):
+            ctx = work.tile([P, HALF], BF16, name=f"ctx{half}")
+            if half == 0:
+                nc.vector.tensor_copy(ctx[:], flipped[:])
+            else:
+                nc.scalar.copy(ctx[:], flipped[:])
             return ctx
 
         def project_out(ctx):
-            result = bank([P, CHUNK], F32, "result")
+            result = bank([P, HALF], F32, "result")
             nc.tensor.matmul(result[:], weights["wo"][:], ctx[:], start=True, stop=True)
             return result
 
-        def store(c, result):
-            out_sb = work.tile([P, CHUNK], F32, name="out_sb")
-            nc.scalar.copy(out_sb[:], result[:])
-            nc.sync.dma_start(out[:, chunk_cols(c)], out_sb[:])
+        def store(c, half, result):
+            out_sb = work.tile([P, HALF], F32, name=f"out_sb{half}")
+            if half == 0:
+                nc.vector.tensor_copy(out_sb[:], result[:])
+            else:
+                nc.scalar.copy(out_sb[:], result[:])
+            first = c * CHUNK + half * HALF
+            nc.sync.dma_start(out[:, first : first + HALF], out_sb[:])
 
         def chunk_done(step, after):
             c, t = divmod(step - AHEAD - after, N_BLOCKS)
@@ -197,7 +208,7 @@ def tile_batchprogramclassifier_b_kernel(tc, table, wc, bc, wq, wk, wv, wo, mask
         nc.scalar.copy(k[:, chunk_cols(0)], project("wk", 0)[:])
         keep_v(0, project_v(0))
         e_tiles, sums, ctx_t, flipped, ctx, result, v_ps, q_ps = {}, {}, {}, {}, {}, {}, {}, {}
-        for step in range(N_TILES + AHEAD + STORE_AFTER):
+        for step in range(N_TILES + AHEAD + STORE_AFTER + 1):
             if step < N_TILES:
                 c, t = divmod(step, N_BLOCKS)
                 coming = t // BLOCKS + 1
@@ -220,18 +231,19 @@ def tile_batchprogramclassifier_b_kernel(tc, table, wc, bc, wq, wk, wv, wo, mask
                     sums[c] = [bank([P, PER_BANK, V_ONE], F32, f"sums{h}") for h in range(BLOCKS // PER_BANK)]
                 attend(c, t, e_tiles[step - AHEAD], sums[c])
 
-            c = chunk_done(step, NORMALISE_AFTER)
-            if c is not None:
-                ctx_t[c] = normalise(sums[c])
-            c = chunk_done(step, FLIP_AFTER)
-            if c is not None:
-                flipped[c] = flip(ctx_t[c])
-            c = chunk_done(step, UNLOAD_AFTER)
-            if c is not None:
-                ctx[c] = unload(flipped[c])
-            c = chunk_done(step, PROJECT_AFTER)
-            if c is not None:
-                result[c] = project_out(ctx[c])
-            c = chunk_done(step, STORE_AFTER)
-            if c is not None:
-                store(c, result[c])
+            for half in range(BLOCKS // PER_BANK):
+                c = chunk_done(step, NORMALISE_AFTER + half)
+                if c is not None:
+                    ctx_t[c, half] = normalise(half, sums[c][half])
+                c = chunk_done(step, FLIP_AFTER + half)
+                if c is not None:
+                    flipped[c, half] = flip(ctx_t[c, half])
+                c = chunk_done(step, UNLOAD_AFTER + half)
+                if c is not None:
+                    ctx[c, half] = unload(half, flipped[c, half])
+                c = chunk_done(step, PROJECT_AFTER + half)
+                if c is not None:
+                    result[c, half] = project_out(ctx[c, half])
+                c = chunk_done(step, STORE_AFTER + half)
+                if c is not None:
+                    store(c, half, result[c, half])

@@ -37,6 +37,9 @@ PROJECT_AFTER = 6
 STORE_AFTER = 7
 COPY_AFTER = 2
 
+SCALE = 1.0 / math.sqrt(P)
+SHIFT = 2048.0
+
 FLOPS = 2 * P * P * NODES * L + 3 * 2 * P * P * L + 2 * 2 * P * L * L + 2 * P * P * L
 
 
@@ -75,6 +78,10 @@ def tile_batchprogramclassifier_b_kernel(tc, table, wc, bc, wq, wk, wv, wo, mask
 
         identity = held.tile([P, P], BF16, name="identity")
         make_identity(nc, identity[:])
+        shift_identity = held.tile([P, P], BF16, name="shift_identity")
+        nc.vector.tensor_scalar_mul(shift_identity[:], identity[:], SHIFT)
+        minus_shift = held.tile([P, 1], F32, name="minus_shift")
+        nc.vector.memset(minus_shift[:], -SCALE * SHIFT)
 
         enc = held.tile([P, L], BF16, name="enc")
         q = held.tile([P, L], BF16, name="q")
@@ -132,16 +139,29 @@ def tile_batchprogramclassifier_b_kernel(tc, table, wc, bc, wq, wk, wv, wo, mask
         def keep_v(c, v_t):
             nc.vector.tensor_copy(v_one[:, c * BLOCKS : (c + 1) * BLOCKS, 0:P], v_t[:])
 
+        def masked_on_tensor(t):
+            return t == N_BLOCKS - 1
+
         def exp_scores(c, t):
             scores = bank([P, CHUNK], F32, "scores")
-            nc.tensor.matmul(scores[:], k[:, t * P : (t + 1) * P], q[:, chunk_cols(c)], start=True, stop=True)
+            keys = k[:, t * P : (t + 1) * P]
             e = probs.tile([P, CHUNK], BF16, name="e")
-            nc.scalar.activation(e[:], scores[:], EXP, scale=1.0 / math.sqrt(P))
+            if masked_on_tensor(t):
+                mask_bf16 = mask_sb[c][t // BLOCKS][:, t % BLOCKS, :].bitcast(BF16).rearrange("p (l h) -> p l h", h=2)
+                nc.tensor.matmul(scores[:], keys, q[:, chunk_cols(c)], start=True, stop=False)
+                nc.tensor.matmul(scores[:], shift_identity[:], mask_bf16[:, :, 1], start=False, stop=True)
+                nc.scalar.activation(e[:], scores[:], EXP, scale=SCALE, bias=minus_shift[:, 0:1])
+            else:
+                nc.tensor.matmul(scores[:], keys, q[:, chunk_cols(c)], start=True, stop=True)
+                nc.scalar.activation(e[:], scores[:], EXP, scale=SCALE)
             return e
 
         def attend(c, t, e, sums):
-            p = probs.tile([P, CHUNK], BF16, name="p")
-            nc.vector.tensor_tensor(p[:], e[:], mask_sb[c][t // BLOCKS][:, t % BLOCKS, :], MULT)
+            if masked_on_tensor(t):
+                p = e
+            else:
+                p = probs.tile([P, CHUNK], BF16, name="p")
+                nc.vector.tensor_tensor(p[:], e[:], mask_sb[c][t // BLOCKS][:, t % BLOCKS, :], MULT)
             for b in range(BLOCKS):
                 half, place = divmod(b, PER_BANK)
                 nc.tensor.matmul(

@@ -139,14 +139,14 @@ def tile_batchprogramclassifier_b_kernel(tc, table, wc, bc, wq, wk, wv, wo, mask
         def keep_v(c, v_t):
             nc.vector.tensor_copy(v_one[:, c * BLOCKS : (c + 1) * BLOCKS, 0:P], v_t[:])
 
-        def masked_on_tensor(t):
-            return t == N_BLOCKS - 1
+        def masked_on_tensor(c, t):
+            return (c == 0 and t < BLOCKS) or (c == N_CHUNKS - 1 and t == N_BLOCKS - 1)
 
         def exp_scores(c, t):
             scores = bank([P, CHUNK], F32, "scores")
             keys = k[:, t * P : (t + 1) * P]
             e = probs.tile([P, CHUNK], BF16, name="e")
-            if masked_on_tensor(t):
+            if masked_on_tensor(c, t):
                 mask_bf16 = mask_sb[c][t // BLOCKS][:, t % BLOCKS, :].bitcast(BF16).rearrange("p (l h) -> p l h", h=2)
                 nc.tensor.matmul(scores[:], keys, q[:, chunk_cols(c)], start=True, stop=False)
                 nc.tensor.matmul(scores[:], shift_identity[:], mask_bf16[:, :, 1], start=False, stop=True)
@@ -157,7 +157,7 @@ def tile_batchprogramclassifier_b_kernel(tc, table, wc, bc, wq, wk, wv, wo, mask
             return e
 
         def attend(c, t, e, sums):
-            if masked_on_tensor(t):
+            if masked_on_tensor(c, t):
                 p = e
             else:
                 p = probs.tile([P, CHUNK], BF16, name="p")

@@ -48,7 +48,9 @@ def tile_batchprogramclassifier_b_kernel(tc, table, wc, bc, wq, wk, wv, wo, mask
     with (
         tc.tile_pool(name="held", bufs=1) as held,
         tc.tile_pool(name="work", bufs=2) as work,
+        tc.tile_pool(name="shifts", bufs=3) as shifts,
         tc.tile_pool(name="probs", bufs=AHEAD + 2) as probs,
+        tc.tile_pool(name="products", bufs=3) as products,
         tc.psum_pool(name="banks", bufs=8) as banks,
     ):
         offsets = held.tile([P, NODES * L // 16], U16, name="offsets")
@@ -139,29 +141,44 @@ def tile_batchprogramclassifier_b_kernel(tc, table, wc, bc, wq, wk, wv, wo, mask
         def keep_v(c, v_t):
             nc.vector.tensor_copy(v_one[:, c * BLOCKS : (c + 1) * BLOCKS, 0:P], v_t[:])
 
-        def masked_on_tensor(c, t):
-            return (c == 0 and t < BLOCKS) or (c == N_CHUNKS - 1 and t == N_BLOCKS - 1)
+        def mask_of(c, t):
+            return mask_sb[c][t // BLOCKS][:, t % BLOCKS, :]
 
-        def exp_scores(c, t):
+        def masked_by(c, t):
+            if (c == 0 and t < BLOCKS) or (c == N_CHUNKS - 1 and t == N_BLOCKS - 1):
+                return "tensor"
+            return "gpsimd" if (c * N_BLOCKS + t) % 3 == 0 else "vector"
+
+        def raw_scores(c, t):
             scores = bank([P, CHUNK], F32, "scores")
             keys = k[:, t * P : (t + 1) * P]
-            e = probs.tile([P, CHUNK], BF16, name="e")
-            if masked_on_tensor(c, t):
-                mask_bf16 = mask_sb[c][t // BLOCKS][:, t % BLOCKS, :].bitcast(BF16).rearrange("p (l h) -> p l h", h=2)
+            if masked_by(c, t) == "tensor":
+                mask_bf16 = mask_of(c, t).bitcast(BF16).rearrange("p (l h) -> p l h", h=2)
                 nc.tensor.matmul(scores[:], keys, q[:, chunk_cols(c)], start=True, stop=False)
                 nc.tensor.matmul(scores[:], shift_identity[:], mask_bf16[:, :, 1], start=False, stop=True)
-                nc.scalar.activation(e[:], scores[:], EXP, scale=SCALE, bias=minus_shift[:, 0:1])
             else:
                 nc.tensor.matmul(scores[:], keys, q[:, chunk_cols(c)], start=True, stop=True)
-                nc.scalar.activation(e[:], scores[:], EXP, scale=SCALE)
+            return scores
+
+        def shift_and_mask(c, t, scores):
+            shifted = shifts.tile([P, CHUNK], F32, name="shifted")
+            nc.vector.scalar_tensor_tensor(shifted[:], scores[:], SHIFT, mask_of(c, t), ADD, MULT)
+            return shifted
+
+        def exponential(c, t, source):
+            e = probs.tile([P, CHUNK], BF16, name="e")
+            if masked_by(c, t) == "gpsimd":
+                nc.scalar.activation(e[:], source[:], EXP, scale=SCALE)
+            else:
+                nc.scalar.activation(e[:], source[:], EXP, scale=SCALE, bias=minus_shift[:, 0:1])
             return e
 
-        def attend(c, t, e, sums):
-            if masked_on_tensor(c, t):
-                p = e
-            else:
-                p = probs.tile([P, CHUNK], BF16, name="p")
-                nc.vector.tensor_tensor(p[:], e[:], mask_sb[c][t // BLOCKS][:, t % BLOCKS, :], MULT)
+        def mask_product(c, t, e):
+            p = products.tile([P, CHUNK], BF16, name="p")
+            nc.gpsimd.tensor_tensor(p[:], e[:], mask_of(c, t), MULT)
+            return p
+
+        def attend(c, t, p, sums):
             for b in range(BLOCKS):
                 half, place = divmod(b, PER_BANK)
                 nc.tensor.matmul(
@@ -227,29 +244,43 @@ def tile_batchprogramclassifier_b_kernel(tc, table, wc, bc, wq, wk, wv, wo, mask
         nc.scalar.copy(q[:, chunk_cols(0)], project("wq", 0)[:])
         nc.scalar.copy(k[:, chunk_cols(0)], project("wk", 0)[:])
         keep_v(0, project_v(0))
-        e_tiles, sums, ctx_t, flipped, ctx, result, v_ps, q_ps = {}, {}, {}, {}, {}, {}, {}, {}
+        nc.scalar.copy(k[:, chunk_cols(1)], project("wk", 1)[:])
+        source, p_tiles, sums, ctx_t, flipped, ctx, result, v_ps, q_ps, k_ps = {}, {}, {}, {}, {}, {}, {}, {}, {}, {}
         for step in range(N_TILES + AHEAD + STORE_AFTER + 1):
             if step < N_TILES:
                 c, t = divmod(step, N_BLOCKS)
                 coming = t // BLOCKS + 1
                 if c == 0 and coming < N_CHUNKS:
                     if t % BLOCKS == 0:
-                        nc.scalar.copy(k[:, chunk_cols(coming)], project("wk", coming)[:])
+                        if coming > 1:
+                            k_ps[coming] = project("wk", coming)
                         v_ps[coming] = project_v(coming)
                     if t % BLOCKS == COPY_AFTER:
+                        if coming > 1:
+                            nc.vector.tensor_copy(k[:, chunk_cols(coming)], k_ps[coming][:])
                         keep_v(coming, v_ps[coming])
                 if c + 1 < N_CHUNKS:
                     if t == N_BLOCKS // 2:
                         q_ps[c + 1] = project("wq", c + 1)
                     if t == N_BLOCKS // 2 + COPY_AFTER:
                         nc.vector.tensor_copy(q[:, chunk_cols(c + 1)], q_ps[c + 1][:])
-                e_tiles[step] = exp_scores(c, t)
+                source[step] = raw_scores(c, t)
+
+            c, t = divmod(step - 1, N_BLOCKS)
+            if 0 <= c < N_CHUNKS and masked_by(c, t) == "vector":
+                source[step - 1] = shift_and_mask(c, t, source[step - 1])
+            c, t = divmod(step - 2, N_BLOCKS)
+            if 0 <= c < N_CHUNKS:
+                p_tiles[step - 2] = exponential(c, t, source[step - 2])
+            c, t = divmod(step - 3, N_BLOCKS)
+            if 0 <= c < N_CHUNKS and masked_by(c, t) == "gpsimd":
+                p_tiles[step - 3] = mask_product(c, t, p_tiles[step - 3])
 
             c, t = divmod(step - AHEAD, N_BLOCKS)
             if 0 <= c < N_CHUNKS:
                 if t == 0:
                     sums[c] = [bank([P, PER_BANK, V_ONE], F32, f"sums{h}") for h in range(BLOCKS // PER_BANK)]
-                attend(c, t, e_tiles[step - AHEAD], sums[c])
+                attend(c, t, p_tiles[step - AHEAD], sums[c])
 
             for half in range(BLOCKS // PER_BANK):
                 c = chunk_done(step, NORMALISE_AFTER + half)

@@ -12,7 +12,6 @@ MULT = mybir.AluOpType.mult
 IDENTITY = mybir.ActivationFunctionType.Identity
 EXP = mybir.ActivationFunctionType.Exp
 RELU = mybir.ActivationFunctionType.Relu
-COPY = mybir.ActivationFunctionType.Copy
 
 P = 128
 V = 4096
@@ -145,7 +144,7 @@ def tile_batchprogramclassifier_b_kernel(tc, table, wc, bc, wq, wk, wv, wo, mask
             return mask_sb[c][t // BLOCKS][:, t % BLOCKS, :]
 
         def masked_by(c, t):
-            if (c == 0 and t < BLOCKS) or (c == N_CHUNKS - 1 and t == N_BLOCKS - 1):
+            if c == N_CHUNKS - 1 and t == N_BLOCKS - 1:
                 return "tensor"
             return "gpsimd" if (c * N_BLOCKS + t) % 3 == 0 else "vector"
 
@@ -193,13 +192,7 @@ def tile_batchprogramclassifier_b_kernel(tc, table, wc, bc, wq, wk, wv, wo, mask
             ctx_t = work.tile([P, PER_BANK, P], BF16, name=f"ctx_t{half}")
             inv_den = work.tile([P, PER_BANK, 1], F32, name=f"inv_den{half}")
             nc.vector.reciprocal(inv_den[:], bank_sums[:, :, P:V_ONE])
-            if half == 0:
-                nc.vector.tensor_tensor(
-                    ctx_t[:], bank_sums[:, :, 0:P], inv_den[:].to_broadcast([P, PER_BANK, P]), MULT
-                )
-            else:
-                for place in range(PER_BANK):
-                    nc.scalar.activation(ctx_t[:, place, :], bank_sums[:, place, 0:P], COPY, scale=inv_den[:, place, :])
+            nc.vector.tensor_tensor(ctx_t[:], bank_sums[:, :, 0:P], inv_den[:].to_broadcast([P, PER_BANK, P]), MULT)
             return ctx_t
 
         def flip(ctx_t):
@@ -210,10 +203,7 @@ def tile_batchprogramclassifier_b_kernel(tc, table, wc, bc, wq, wk, wv, wo, mask
 
         def unload(half, flipped):
             ctx = work.tile([P, HALF], BF16, name=f"ctx{half}")
-            if half == 0:
-                nc.vector.tensor_copy(ctx[:], flipped[:])
-            else:
-                nc.scalar.copy(ctx[:], flipped[:])
+            nc.vector.tensor_copy(ctx[:], flipped[:])
             return ctx
 
         def project_out(ctx):

@@ -30,10 +30,10 @@ PER_BANK = 2
 
 AHEAD = 7
 NORMALISE_AFTER = 2
-FLIP_AFTER = 3
-UNLOAD_AFTER = 5
-PROJECT_AFTER = 6
-STORE_AFTER = 7
+FLIP_AFTER = 4
+UNLOAD_AFTER = 6
+PROJECT_AFTER = 8
+STORE_AFTER = 10
 COPY_AFTER = 2
 
 SCALE = 1.0 / math.sqrt(P)

import math

import concourse.mybir as mybir
from concourse.masks import make_identity

BF16 = mybir.dt.bfloat16
F32 = mybir.dt.float32
U16 = mybir.dt.uint16
ADD = mybir.AluOpType.add
MAX = mybir.AluOpType.max
MULT = mybir.AluOpType.mult
IDENTITY = mybir.ActivationFunctionType.Identity
EXP = mybir.ActivationFunctionType.Exp
RELU = mybir.ActivationFunctionType.Relu

P = 128
V = 4096
L = 2048
NODES = 3
CHUNK = 512
N_CHUNKS = L // CHUNK
BLOCKS = CHUNK // P
N_BLOCKS = L // P
OFFS_COLS = CHUNK // 16
V_ONE = P + 1
N_TILES = N_CHUNKS * N_BLOCKS
V_PITCH = 144
HALF = 2 * P
PER_BANK = 2

AHEAD = 7
NORMALISE_AFTER = 2
FLIP_AFTER = 4
UNLOAD_AFTER = 6
PROJECT_AFTER = 8
STORE_AFTER = 10
COPY_AFTER = 2

SCALE = 1.0 / math.sqrt(P)
SHIFT = 2048.0

FLOPS = 2 * P * P * NODES * L + 3 * 2 * P * P * L + 2 * 2 * P * L * L + 2 * P * P * L


def tile_batchprogramclassifier_b_kernel(tc, table, wc, bc, wq, wk, wv, wo, mask, offs, out):
    nc = tc.nc
    with (
        tc.tile_pool(name="held", bufs=1) as held,
        tc.tile_pool(name="work", bufs=2) as work,
        tc.tile_pool(name="shifts", bufs=3) as shifts,
        tc.tile_pool(name="probs", bufs=AHEAD + 2) as probs,
        tc.tile_pool(name="products", bufs=3) as products,
        tc.psum_pool(name="banks", bufs=8) as banks,
    ):
        offsets = held.tile([P, NODES * L // 16], U16, name="offsets")
        nc.sync.dma_start(offsets[:], offs)
        table_sb = held.tile([P, V], BF16, name="table_sb")
        nc.sync.dma_start(table_sb[:], table)

        weights = {}
        for name, w in (("wc", wc), ("wq", wq), ("wk", wk), ("wv", wv), ("wo", wo)):
            weights[name] = held.tile([P, P], BF16, name=name + "_sb")
            nc.scalar.dma_start(weights[name][:], w)
        bc_sb = held.tile([P, 1], F32, name="bc_sb")
        nc.scalar.dma_start(bc_sb[:], bc)

        warm = held.tile([P, 1], F32, name="warm")
        nc.vector.memset(warm[:], 0.0)
        nc.scalar.activation(warm[:], warm[:], EXP)

        mask_view = mask.rearrange("(g j p) l -> g p j l", j=BLOCKS, p=P)
        mask_sb = []
        for c in range(N_CHUNKS):
            mask_sb.append([])
            for g in range(N_BLOCKS // BLOCKS):
                m_tile = held.tile([P, BLOCKS, CHUNK], F32, name=f"mask_{c}_{g}")
                nc.sync.dma_start(m_tile[:], mask_view[g, :, :, c * CHUNK : (c + 1) * CHUNK])
                mask_sb[c].append(m_tile)

        identity = held.tile([P, P], BF16, name="identity")
        make_identity(nc, identity[:])
        shift_identity = held.tile([P, P], BF16, name="shift_identity")
        nc.vector.tensor_scalar_mul(shift_identity[:], identity[:], SHIFT)
        minus_shift = held.tile([P, 1], F32, name="minus_shift")
        nc.vector.memset(minus_shift[:], -SCALE * SHIFT)

        enc = held.tile([P, L], BF16, name="enc")
        q = held.tile([P, L], BF16, name="q")
        k = held.tile([P, L], BF16, name="k")
        v_one = held.tile([P, N_BLOCKS, V_PITCH], BF16, name="v_one")
        nc.vector.memset(v_one[:, :, P:V_ONE], 1.0)

        def chunk_cols(c):
            return slice(c * CHUNK, (c + 1) * CHUNK)

        def bank(shape, dtype, name):
            return banks.tile(shape, dtype, name=name, tag="bank")

        def embed(c):
            raw = {}
            for node in (1, 2, 0):
                piece = node * N_CHUNKS + c
                raw[node] = bank([P, CHUNK], F32, f"raw{node}")
                nc.tensor.matmul(
                    raw[node][:],
                    weights["wc"][:],
                    table_sb[:].indirect(offsets[:, piece * OFFS_COLS : (piece + 1) * OFFS_COLS]),
                    start=True,
                    stop=True,
                )
            return raw

        def pool_trees(c, raw):
            left = work.tile([P, CHUNK], F32, name="left")
            nc.scalar.activation(left[:], raw[1][:], IDENTITY, bias=bc_sb[:, 0:1])
            left_or_zero = work.tile([P, CHUNK], BF16, name="left_or_zero")
            nc.scalar.activation(left_or_zero[:], raw[1][:], RELU, bias=bc_sb[:, 0:1])
            children = work.tile([P, CHUNK], F32, name="children")
            nc.vector.scalar_tensor_tensor(children[:], raw[2][:], bc_sb[:, 0:1], left[:], ADD, ADD)
            biggest = work.tile([P, CHUNK], BF16, name="biggest")
            nc.vector.scalar_tensor_tensor(biggest[:], raw[2][:], bc_sb[:, 0:1], left_or_zero[:], ADD, MAX)
            subtree = work.tile([P, CHUNK], BF16, name="subtree")
            nc.vector.scalar_tensor_tensor(subtree[:], raw[0][:], bc_sb[:, 0:1], children[:], ADD, ADD)
            nc.vector.tensor_tensor(enc[:, chunk_cols(c)], subtree[:], biggest[:], MAX)

        def project(w_name, c):
            proj = bank([P, CHUNK], BF16, "proj")
            nc.tensor.matmul(proj[:], weights[w_name][:], enc[:, chunk_cols(c)], start=True, stop=True)
            return proj

        def project_v(c):
            v_t = bank([P, BLOCKS, P], BF16, "v_t")
            for j in range(BLOCKS):
                block = c * BLOCKS + j
                nc.tensor.matmul(
                    v_t[:, j, :], enc[:, block * P : (block + 1) * P], weights["wv"][:], start=True, stop=True
                )
            return v_t

        def keep_v(c, v_t):
            nc.vector.tensor_copy(v_one[:, c * BLOCKS : (c + 1) * BLOCKS, 0:P], v_t[:])

        def mask_of(c, t):
            return mask_sb[c][t // BLOCKS][:, t % BLOCKS, :]

        def masked_by(c, t):
            if c == N_CHUNKS - 1 and t == N_BLOCKS - 1:
                return "tensor"
            return "gpsimd" if (c * N_BLOCKS + t) % 3 == 0 else "vector"

        def raw_scores(c, t):
            scores = bank([P, CHUNK], F32, "scores")
            keys = k[:, t * P : (t + 1) * P]
            if masked_by(c, t) == "tensor":
                mask_bf16 = mask_of(c, t).bitcast(BF16).rearrange("p (l h) -> p l h", h=2)
                nc.tensor.matmul(scores[:], keys, q[:, chunk_cols(c)], start=True, stop=False)
                nc.tensor.matmul(scores[:], shift_identity[:], mask_bf16[:, :, 1], start=False, stop=True)
            else:
                nc.tensor.matmul(scores[:], keys, q[:, chunk_cols(c)], start=True, stop=True)
            return scores

        def shift_and_mask(c, t, scores):
            shifted = shifts.tile([P, CHUNK], F32, name="shifted")
            nc.vector.scalar_tensor_tensor(shifted[:], scores[:], SHIFT, mask_of(c, t), ADD, MULT)
            return shifted

        def exponential(c, t, source):
            e = probs.tile([P, CHUNK], BF16, name="e")
            if masked_by(c, t) == "gpsimd":
                nc.scalar.activation(e[:], source[:], EXP, scale=SCALE)
            else:
                nc.scalar.activation(e[:], source[:], EXP, scale=SCALE, bias=minus_shift[:, 0:1])
            return e

        def mask_product(c, t, e):
            p = products.tile([P, CHUNK], BF16, name="p")
            nc.gpsimd.tensor_tensor(p[:], e[:], mask_of(c, t), MULT)
            return p

        def attend(c, t, p, sums):
            for b in range(BLOCKS):
                half, place = divmod(b, PER_BANK)
                nc.tensor.matmul(
                    sums[half][:, place, :],
                    p[:, b * P : (b + 1) * P],
                    v_one[:, t, 0:V_ONE],
                    start=(t == 0 and place == 0),
                    stop=(t == N_BLOCKS - 1 and place == PER_BANK - 1),
                )

        def normalise(half, bank_sums):
            ctx_t = work.tile([P, PER_BANK, P], BF16, name=f"ctx_t{half}")
            inv_den = work.tile([P, PER_BANK, 1], F32, name=f"inv_den{half}")
            nc.vector.reciprocal(inv_den[:], bank_sums[:, :, P:V_ONE])
            nc.vector.tensor_tensor(ctx_t[:], bank_sums[:, :, 0:P], inv_den[:].to_broadcast([P, PER_BANK, P]), MULT)
            return ctx_t

        def flip(ctx_t):
            flipped = bank([P, HALF], BF16, "flipped")
            for place in range(PER_BANK):
                nc.tensor.transpose(flipped[:, place * P : (place + 1) * P], ctx_t[:, place, :], identity[:])
            return flipped

        def unload(half, flipped):
            ctx = work.tile([P, HALF], BF16, name=f"ctx{half}")
            nc.vector.tensor_copy(ctx[:], flipped[:])
            return ctx

        def project_out(ctx):
            result = bank([P, HALF], F32, "result")
            nc.tensor.matmul(result[:], weights["wo"][:], ctx[:], start=True, stop=True)
            return result

        def store(c, half, result):
            out_sb = work.tile([P, HALF], F32, name=f"out_sb{half}")
            if half == 0:
                nc.vector.tensor_copy(out_sb[:], result[:])
            else:
                nc.scalar.copy(out_sb[:], result[:])
            first = c * CHUNK + half * HALF
            nc.sync.dma_start(out[:, first : first + HALF], out_sb[:])

        def chunk_done(step, after):
            c, t = divmod(step - AHEAD - after, N_BLOCKS)
            return c if t == N_BLOCKS - 1 and 0 <= c < N_CHUNKS else None

        raw = {}
        for c in range(N_CHUNKS + 1):
            if c < N_CHUNKS:
                raw[c] = embed(c)
            if c >= 1:
                pool_trees(c - 1, raw[c - 1])

        nc.scalar.copy(q[:, chunk_cols(0)], project("wq", 0)[:])
        nc.scalar.copy(k[:, chunk_cols(0)], project("wk", 0)[:])
        keep_v(0, project_v(0))
        nc.scalar.copy(k[:, chunk_cols(1)], project("wk", 1)[:])
        source, p_tiles, sums, ctx_t, flipped, ctx, result, v_ps, q_ps, k_ps = {}, {}, {}, {}, {}, {}, {}, {}, {}, {}
        for step in range(N_TILES + AHEAD + STORE_AFTER + 1):
            if step < N_TILES:
                c, t = divmod(step, N_BLOCKS)
                coming = t // BLOCKS + 1
                if c == 0 and coming < N_CHUNKS:
                    if t % BLOCKS == 0:
                        if coming > 1:
                            k_ps[coming] = project("wk", coming)
                        v_ps[coming] = project_v(coming)
                    if t % BLOCKS == COPY_AFTER:
                        if coming > 1:
                            nc.vector.tensor_copy(k[:, chunk_cols(coming)], k_ps[coming][:])
                        keep_v(coming, v_ps[coming])
                if c + 1 < N_CHUNKS:
                    if t == N_BLOCKS // 2:
                        q_ps[c + 1] = project("wq", c + 1)
                    if t == N_BLOCKS // 2 + COPY_AFTER:
                        nc.vector.tensor_copy(q[:, chunk_cols(c + 1)], q_ps[c + 1][:])
                source[step] = raw_scores(c, t)

            c, t = divmod(step - 1, N_BLOCKS)
            if 0 <= c < N_CHUNKS and masked_by(c, t) == "vector":
                source[step - 1] = shift_and_mask(c, t, source[step - 1])
            c, t = divmod(step - 2, N_BLOCKS)
            if 0 <= c < N_CHUNKS:
                p_tiles[step - 2] = exponential(c, t, source[step - 2])
            c, t = divmod(step - 3, N_BLOCKS)
            if 0 <= c < N_CHUNKS and masked_by(c, t) == "gpsimd":
                p_tiles[step - 3] = mask_product(c, t, p_tiles[step - 3])

            c, t = divmod(step - AHEAD, N_BLOCKS)
            if 0 <= c < N_CHUNKS:
                if t == 0:
                    sums[c] = [bank([P, PER_BANK, V_ONE], F32, f"sums{h}") for h in range(BLOCKS // PER_BANK)]
                attend(c, t, p_tiles[step - AHEAD], sums[c])

            for half in range(BLOCKS // PER_BANK):
                c = chunk_done(step, NORMALISE_AFTER + half)
                if c is not None:
                    ctx_t[c, half] = normalise(half, sums[c][half])
                c = chunk_done(step, FLIP_AFTER + half)
                if c is not None:
                    flipped[c, half] = flip(ctx_t[c, half])
                c = chunk_done(step, UNLOAD_AFTER + half)
                if c is not None:
                    ctx[c, half] = unload(half, flipped[c, half])
                c = chunk_done(step, PROJECT_AFTER + half)
                if c is not None:
                    result[c, half] = project_out(ctx[c, half])
                c = chunk_done(step, STORE_AFTER + half)
                if c is not None:
                    store(c, half, result[c, half])
